import numpy as np
import ml_dtypes


def mxq(x, axis, fmt="e4m3"):
    dtype, down = {"e4m3": (ml_dtypes.float8_e4m3fn, 7), "e5m2": (ml_dtypes.float8_e5m2, 14)}[fmt]
    v = np.moveaxis(np.asarray(x, np.float32).astype(ml_dtypes.bfloat16).astype(np.float64), axis, -1)
    blocks = v.reshape(v.shape[:-1] + (-1, 32))
    amax = np.abs(blocks).max(-1, keepdims=True)
    byte = np.maximum(np.where(amax > 0, np.frexp(amax)[1] - 1 + 127, 0) - down, 1)
    scale = np.exp2(byte - 127.0)
    codes = (blocks / scale).astype(np.float32).astype(dtype).astype(np.float64)
    return np.moveaxis((codes * scale).reshape(v.shape), -1, axis)


WIDE = False


def mx_kscale(k):
    if not WIDE:
        return np.ones(k)
    levels = np.array([10, -10, 5, -5, 0])
    a = np.random.permutation(np.resize(levels, k // 512 * 4)).reshape(k // 512, 4)
    idx = np.arange(k)
    return np.exp2(a[idx // 512, idx % 128 // 32])


BF16 = ml_dtypes.bfloat16


def bf(x):
    return np.asarray(x, np.float32).astype(BF16)


def f64(x):
    return np.asarray(x).astype(np.float64)


B, A, G, H1, H2 = 1024, 128, 5, 2048, 2048
SLOPE = 0.4


def leaky(v):
    return np.where(v >= 0.0, v, SLOPE * v)


def setup_inputs():
    s, t = mx_kscale(H1), mx_kscale(H2)
    keep = np.where(np.random.uniform(size=(B, A)) > 0.2, 1.0, 0.0)
    return {"x": bf(np.random.standard_normal((B, A * G)) * np.repeat(keep, G, axis=1)),
            "h1": bf(leaky(np.random.standard_normal((B, H1))) * s),
            "W2": bf(np.random.standard_normal((H1, H2)) * 1.3 / np.sqrt(H1) / s[:, None] * t),
            "b2": bf(np.random.standard_normal(H2) * 0.3 * t),
            "W3": bf(np.random.standard_normal((H2, A)) * 2.5 / np.sqrt(H2) / t[:, None]),
            "b3": bf(np.random.standard_normal(A) * 0.5)}


def reference(x, h1, W2, b2, W3, b3):
    gsum = f64(x).reshape(B, A, G).sum(axis=-1)
    mask = gsum != 0.0
    h2 = leaky((mxq(f64(h1), 1, "e4m3") @ mxq(f64(W2), 0, "e4m3")) + f64(b2))
    logits = (mxq(h2, 1, "e4m3") @ mxq(f64(W3), 0, "e4m3")) + f64(b3)
    logits = np.where(mask, logits, -np.inf)
    e = np.exp(logits - logits.max(axis=1, keepdims=True))
    return e / e.sum(axis=1, keepdims=True)

@@ -1,0 +1,230 @@
+from contextlib import ExitStack
+
+import concourse.mybir as mybir
+from concourse.masks import make_identity
+
+F32 = mybir.dt.float32
+BF16 = mybir.dt.bfloat16
+U32 = mybir.dt.uint32
+U8 = mybir.dt.uint8
+FP8X4 = mybir.dt.float8_e4m3fn_x4
+ALU = mybir.AluOpType
+ACT = mybir.ActivationFunctionType
+AX = mybir.AxisListType
+
+P = 128
+B, A, G, H1, H2 = 1024, 128, 5, 2048, 2048
+SLOPE = 0.4
+BIG = 1.0e30
+FLOPS = 2 * B * H1 * H2 + 2 * B * H2 * A
+
+WV = 224
+RAW_BUFS = 12
+
+
+def tile_dqn_pa_kernel(tc, x, h1, W2, b2, W3, b3, out):
+    nc = tc.nc
+    with ExitStack() as ctx:
+        const = ctx.enter_context(tc.tile_pool(name="const", bufs=1))
+        raw = ctx.enter_context(tc.tile_pool(name="raw", bufs=RAW_BUFS))
+        h1gp = ctx.enter_context(tc.tile_pool(name="h1gp", bufs=3))
+        w2gp = ctx.enter_context(tc.tile_pool(name="w2gp", bufs=4))
+        apool = ctx.enter_context(tc.tile_pool(name="apool", bufs=2))
+        h2gp = ctx.enter_context(tc.tile_pool(name="h2gp", bufs=2))
+        sm = ctx.enter_context(tc.tile_pool(name="sm", bufs=2))
+        psum = ctx.enter_context(tc.psum_pool(name="psum", bufs=6))
+        lgp = ctx.enter_context(tc.psum_pool(name="lgp", bufs=2))
+
+        ident = const.tile([P, P], F32, name="ident")
+        make_identity(nc, ident[:])
+        warm = const.tile([P, 2], F32, name="warm")
+        nc.vector.memset(warm[:], 0.0)
+        nc.scalar.activation(out=warm[:, 1:2], in_=warm[:, 0:1], func=ACT.Exp)
+        b2rows = const.tile([P, P], BF16, name="b2rows")
+        nc.vector.memset(b2rows[:], 0.0)
+        nc.scalar.dma_start(out=b2rows[0:16, :], in_=b2.rearrange("(m p) -> m p", p=P))
+
+        h1codes = const.tile([P, 4, B], U32, name="h1codes", align_bytes=64)
+        h1sc = const.tile([P, 4, B], U8, name="h1sc", align_bytes=64)
+        w2codes = const.tile([P, 4, H2], U32, name="w2codes", align_bytes=64)
+        w2sc = const.tile([P, 4, H2], U8, name="w2sc", align_bytes=64)
+        h2codes = const.tile([P, 4, B], U32, name="h2codes", align_bytes=64)
+        h2sc = const.tile([P, 4, B], U8, name="h2sc", align_bytes=64)
+        w3codes = const.tile([P, 4 * A], U32, name="w3codes", align_bytes=64)
+        w3sc = const.tile([P, 4 * A], U8, name="w3sc", align_bytes=64)
+
+        xparts = []
+        for (i0, n) in ((0, 3), (3, 3), (6, 2)):
+            t = raw.tile([P, n, A * G], BF16, name="xraw%d" % i0, tag="raw")
+            nc.sync.dma_start(out=t[:], in_=x[i0 * P:(i0 + n) * P, :].rearrange("(i p) c -> p i c", p=P))
+            xparts.append((i0, n, t))
+        b3bc = raw.tile([P, A], BF16, name="b3bc", tag="raw")
+        nc.sync.dma_start(out=b3bc[:], in_=b3.partition_broadcast(P))
+        h1raw = []
+        for i in range(8):
+            t = raw.tile([P, H1], BF16, name="h1raw%d" % i, tag="raw")
+            nc.sync.dma_start(out=t[:], in_=h1[i * P:(i + 1) * P, :])
+            h1raw.append(t)
+        w2raw = {}
+        for g in range(4):
+            for c in range(4):
+                t = raw.tile([P, 4, 512], BF16, name="w2raw%d_%d" % (g, c), tag="raw")
+                for u in range(2):
+                    r0 = 512 * c + 256 * u
+                    nc.sync.dma_start(
+                        out=t[:, 2 * u:2 * u + 2, :],
+                        in_=W2[r0:r0 + 256, 512 * g:512 * g + 512].rearrange("(q e) w -> q e w", e=2),
+                    )
+                w2raw[(g, c)] = t
+        w3raw = raw.tile([P, 16, A], BF16, name="w3raw", tag="raw")
+        nc.sync.dma_start(out=w3raw[:], in_=W3.rearrange("(m p) a -> p m a", p=P))
+
+        def h1_half(bh):
+            units = [
+                h1gp.tile([P, 2 * 512 * 4], BF16, name="h1g%d_%d" % (bh, gp), tag="h1g", align_bytes=64)
+                for gp in range(2)
+            ]
+            for ii in range(4):
+                words = h1raw[4 * bh + ii][:].bitcast(F32)
+                for gp in range(2):
+                    bank = psum.tile([P, 2, 2, P], F32, name="trb%d_%d_%d" % (bh, ii, gp), tag="bank")
+                    for gg in range(2):
+                        for u in range(2):
+                            w0 = 256 * (2 * gp + gg) + 128 * u
+                            nc.tensor.transpose(bank[:, gg, u, :], words[:, w0:w0 + P], ident[:])
+                    dst = units[gp][:].bitcast(F32).rearrange("p (g b u) -> p g b u", g=2, u=2)
+                    dst = dst[:, :, ii * P:(ii + 1) * P, :]
+                    src = bank[:].rearrange("p g u b -> p g b u")
+                    nc.scalar.copy(out=dst, in_=src)
+            for gp in range(2):
+                for gg in range(2):
+                    c = 2 * gp + gg
+                    nc.vector.quantize_mx(
+                        out=h1codes[:, c, 512 * bh:512 * bh + 512].bitcast(FP8X4),
+                        scales=h1sc[:, c, 512 * bh:512 * bh + 512],
+                        in_=units[gp][:, 2048 * gg:2048 * gg + 2048],
+                    )
+
+        def w2_chunk(g, c):
+            src = w2raw[(g, c)]
+            grp = w2gp.tile([P, 512, 4], BF16, name="w2g%d_%d" % (g, c), tag="w2g", align_bytes=64)
+            nc.vector.tensor_copy(
+                out=grp[:, 0:WV, :].rearrange("p (c i) t -> p c t i", i=4),
+                in_=src[:, :, 0:WV].rearrange("p t (c i) -> p c t i", i=4),
+            )
+            nc.scalar.copy(
+                out=grp[:, WV:512, :].rearrange("p (c i) t -> p c t i", i=4),
+                in_=src[:, :, WV:512].rearrange("p t (c i) -> p c t i", i=4),
+            )
+            nc.vector.quantize_mx(
+                out=w2codes[:, c, 512 * g:512 * g + 512].bitcast(FP8X4),
+                scales=w2sc[:, c, 512 * g:512 * g + 512],
+                in_=grp[:].rearrange("p w t -> p (w t)"),
+            )
+
+        def mm1(g, bh, c_outer):
+            banks = [psum.tile([P, 512], F32, name="mm%d_%d_%d" % (g, bh, t), tag="bank") for t in range(4)]
+            if c_outer:
+                order = [(c, t) for c in range(4) for t in range(4)]
+            else:
+                order = [(c, t) for t in range(4) for c in range(4)]
+            for (c, t) in order:
+                m = 4 * g + t
+                nc.tensor.matmul_mx(
+                    out=banks[t][:],
+                    lhsT=w2codes[:, c, m * P:(m + 1) * P].bitcast(FP8X4),
+                    lhsT_scale=w2sc[:, c, m * P:(m + 1) * P],
+                    rhs=h1codes[:, c, 512 * bh:512 * bh + 512].bitcast(FP8X4),
+                    rhs_scale=h1sc[:, c, 512 * bh:512 * bh + 512],
+                    start=(c == 0),
+                    stop=(c == 3),
+                )
+            return banks
+
+        def epilogue(g, bh, banks):
+            a = apool.tile([P, 4, 512], F32, name="a%d_%d" % (g, bh), tag="a")
+            for t in range(4):
+                m = 4 * g + t
+                nc.scalar.activation(out=a[:, t, :], in_=banks[t][:], func=ACT.Identity,
+                                     bias=b2T[:, m:m + 1], scale=1.0)
+            h2g = h2gp.tile([P, 512, 4], BF16, name="h2g%d_%d" % (g, bh), tag="h2g", align_bytes=64)
+            av = a[:].rearrange("p t b -> p b t")
+            nc.vector.scalar_tensor_tensor(out=h2g[:], in0=av, scalar=SLOPE, in1=av,
+                                           op0=ALU.mult, op1=ALU.max)
+            nc.vector.quantize_mx(
+                out=h2codes[:, g, 512 * bh:512 * bh + 512].bitcast(FP8X4),
+                scales=h2sc[:, g, 512 * bh:512 * bh + 512],
+                in_=h2g[:].rearrange("p b t -> p (b t)"),
+            )
+
+        def head(j):
+            lg = lgp.tile([P, 4, A], F32, name="lg%d" % j, tag="lg")
+            for ii in range(4):
+                i = 4 * j + ii
+                for g in range(4):
+                    nc.tensor.matmul_mx(
+                        out=lg[:, ii, :],
+                        lhsT=h2codes[:, g, i * P:(i + 1) * P].bitcast(FP8X4),
+                        lhsT_scale=h2sc[:, g, i * P:(i + 1) * P],
+                        rhs=w3codes[:, g * A:(g + 1) * A].bitcast(FP8X4),
+                        rhs_scale=w3sc[:, g * A:(g + 1) * A],
+                        start=(g == 0),
+                        stop=(g == 3),
+                    )
+            nlp = sm.tile([P, 4, A], F32, name="nlp%d" % j, tag="nlp")
+            nc.vector.tensor_tensor(out=nlp[:], in0=nbm[:, 4 * j:4 * j + 4, :], in1=lg[:], op=ALU.subtract)
+            nmx = sm.tile([P, 4], F32, name="nmx%d" % j, tag="nmx")
+            nc.vector.tensor_reduce(out=nmx[:], in_=nlp[:], axis=AX.X, op=ALU.min)
+            e = sm.tile([P, 4, A], F32, name="e%d" % j, tag="e")
+            s = sm.tile([P, 4], F32, name="s%d" % j, tag="s")
+            for ii in range(4):
+                nc.scalar.activation(out=e[:, ii, :], in_=nlp[:, ii, :], func=ACT.Exp,
+                                     bias=nmx[:, ii:ii + 1], scale=-1.0, accum_out=s[:, ii:ii + 1])
+            r = sm.tile([P, 4], F32, name="r%d" % j, tag="r")
+            nc.vector.reciprocal(out=r[:], in_=s[:])
+            for ii in range(4):
+                nc.scalar.activation(out=e[:, ii, :], in_=e[:, ii, :], func=ACT.Copy, scale=r[:, ii:ii + 1])
+            nc.sync.dma_start(out=out[512 * j:512 * j + 512, :].rearrange("(i p) a -> p i a", p=P), in_=e[:])
+
+        b2rows32 = const.tile([P, P], F32, name="b2rows32")
+        nc.vector.tensor_copy(out=b2rows32[:], in_=b2rows[:])
+        b2ps = psum.tile([P, 512], F32, name="b2ps", tag="bank")
+        nc.tensor.transpose(b2ps[:, 0:P], b2rows32[:], ident[:])
+        b2T = const.tile([P, 16], F32, name="b2T")
+        nc.vector.tensor_copy(out=b2T[:], in_=b2ps[:, 0:16])
+
+        nbm = const.tile([P, 8, A], F32, name="nbm")
+        for (i0, n, t) in xparts:
+            for i in range(n):
+                nc.vector.tensor_reduce(out=nbm[:, i0 + i, :],
+                                        in_=t[:, i, :].rearrange("p (a j) -> p a j", j=G),
+                                        axis=AX.X, op=ALU.add)
+        nc.vector.tensor_scalar(out=nbm[:], in0=nbm[:], scalar1=0.0, scalar2=BIG,
+                                op0=ALU.is_equal, op1=ALU.mult)
+        nc.vector.tensor_tensor(out=nbm[:], in0=nbm[:],
+                                in1=b3bc[:].unsqueeze(1).to_broadcast([P, 8, A]), op=ALU.subtract)
+
+        h1_half(0)
+        h1_half(1)
+
+        for c in range(4):
+            w2_chunk(0, c)
+        for g in range(4):
+            banks0 = mm1(g, 0, g == 0)
+            if g < 3:
+                w2_chunk(g + 1, 0)
+                w2_chunk(g + 1, 1)
+            epilogue(g, 0, banks0)
+            banks1 = mm1(g, 1, False)
+            if g < 3:
+                w2_chunk(g + 1, 2)
+                w2_chunk(g + 1, 3)
+            if g == 2:
+                w3g = const.tile([P, 4, A, 4], BF16, name="w3g", align_bytes=64)
+                nc.vector.tensor_copy(out=w3g[:], in_=w3raw[:].rearrange("p (g t) a -> p g a t", t=4))
+                nc.vector.quantize_mx(out=w3codes[:].bitcast(FP8X4), scales=w3sc[:],
+                                      in_=w3g[:].rearrange("p g a t -> p (g a t)"))
+            epilogue(g, 1, banks1)
+            if g == 3:
+                head(0)
+        head(1)

@@ -18,22 +18,25 @@ SLOPE = 0.4
 BIG = 1.0e30
 FLOPS = 2 * B * H1 * H2 + 2 * B * H2 * A
 
-WV = 224
-RAW_BUFS = 12
+PIN = False
+WVS = (128, 416, 256, 160)
+AHEAD = 14
+EFROM = 9
+UNITS = [(0, 0, 4), (0, 4, 4), (1, 0, 4), (1, 4, 4), (2, 0, 4), (2, 4, 4), (3, 0, 2), (3, 2, 2), (3, 4, 2), (3, 6, 2)]
 
 
 def tile_dqn_pa_kernel(tc, x, h1, W2, b2, W3, b3, out):
     nc = tc.nc
     with ExitStack() as ctx:
         const = ctx.enter_context(tc.tile_pool(name="const", bufs=1))
-        raw = ctx.enter_context(tc.tile_pool(name="raw", bufs=RAW_BUFS))
-        h1gp = ctx.enter_context(tc.tile_pool(name="h1gp", bufs=3))
+        raw = ctx.enter_context(tc.tile_pool(name="raw", bufs=12))
+        big = ctx.enter_context(tc.tile_pool(name="big", bufs=5))
         w2gp = ctx.enter_context(tc.tile_pool(name="w2gp", bufs=4))
-        apool = ctx.enter_context(tc.tile_pool(name="apool", bufs=2))
         h2gp = ctx.enter_context(tc.tile_pool(name="h2gp", bufs=2))
         sm = ctx.enter_context(tc.tile_pool(name="sm", bufs=2))
-        psum = ctx.enter_context(tc.psum_pool(name="psum", bufs=6))
-        lgp = ctx.enter_context(tc.psum_pool(name="lgp", bufs=2))
+        psum = ctx.enter_context(tc.psum_pool(name="psum", bufs=8))
+        if PIN:
+            ctx.enter_context(tc.manual_schedule())
 
         ident = const.tile([P, P], F32, name="ident")
         make_identity(nc, ident[:])
@@ -43,6 +46,11 @@ def tile_dqn_pa_kernel(tc, x, h1, W2, b2, W3, b3, out):
         b2rows = const.tile([P, P], BF16, name="b2rows")
         nc.vector.memset(b2rows[:], 0.0)
         nc.scalar.dma_start(out=b2rows[0:16, :], in_=b2.rearrange("(m p) -> m p", p=P))
+        b3row = const.tile([P, A], BF16, name="b3row")
+        nc.vector.memset(b3row[:], 0.0)
+        nc.scalar.dma_start(out=b3row[0:1, :], in_=b3.rearrange("(o a) -> o a", o=1))
+        ones = const.tile([P, P], BF16, name="ones")
+        nc.vector.memset(ones[:], 1.0)
 
         h1codes = const.tile([P, 4, B], U32, name="h1codes", align_bytes=64)
         h1sc = const.tile([P, 4, B], U8, name="h1sc", align_bytes=64)
@@ -52,179 +60,363 @@ def tile_dqn_pa_kernel(tc, x, h1, W2, b2, W3, b3, out):
         h2sc = const.tile([P, 4, B], U8, name="h2sc", align_bytes=64)
         w3codes = const.tile([P, 4 * A], U32, name="w3codes", align_bytes=64)
         w3sc = const.tile([P, 4 * A], U8, name="w3sc", align_bytes=64)
+        b2rows32 = const.tile([P, P], F32, name="b2rows32")
+        b2T = const.tile([P, 16], F32, name="b2T")
+        b3bc = const.tile([P, A], F32, name="b3bc")
+        nbm = const.tile([P, 8, A], F32, name="nbm")
+        w3g = const.tile([P, 4, A, 4], BF16, name="w3g", align_bytes=64)
 
-        xparts = []
+        xof = {}
         for (i0, n) in ((0, 3), (3, 3), (6, 2)):
             t = raw.tile([P, n, A * G], BF16, name="xraw%d" % i0, tag="raw")
             nc.sync.dma_start(out=t[:], in_=x[i0 * P:(i0 + n) * P, :].rearrange("(i p) c -> p i c", p=P))
-            xparts.append((i0, n, t))
-        b3bc = raw.tile([P, A], BF16, name="b3bc", tag="raw")
-        nc.sync.dma_start(out=b3bc[:], in_=b3.partition_broadcast(P))
+            for i in range(n):
+                xof[i0 + i] = t[:, i, :]
         h1raw = []
         for i in range(8):
             t = raw.tile([P, H1], BF16, name="h1raw%d" % i, tag="raw")
             nc.sync.dma_start(out=t[:], in_=h1[i * P:(i + 1) * P, :])
             h1raw.append(t)
-        w2raw = {}
-        for g in range(4):
-            for c in range(4):
-                t = raw.tile([P, 4, 512], BF16, name="w2raw%d_%d" % (g, c), tag="raw")
-                for u in range(2):
-                    r0 = 512 * c + 256 * u
-                    nc.sync.dma_start(
-                        out=t[:, 2 * u:2 * u + 2, :],
-                        in_=W2[r0:r0 + 256, 512 * g:512 * g + 512].rearrange("(q e) w -> q e w", e=2),
-                    )
-                w2raw[(g, c)] = t
+        w2raw = []
+        for k in range(16):
+            g, c = k // 4, k % 4
+            t = raw.tile([P, 4, 512], BF16, name="w2raw%d" % k, tag="raw")
+            for u in range(2):
+                r0 = 512 * c + 256 * u
+                nc.sync.dma_start(
+                    out=t[:, 2 * u:2 * u + 2, :],
+                    in_=W2[r0:r0 + 256, 512 * g:512 * g + 512].rearrange("(q e) w -> q e w", e=2),
+                )
+            w2raw.append(t)
         w3raw = raw.tile([P, 16, A], BF16, name="w3raw", tag="raw")
         nc.sync.dma_start(out=w3raw[:], in_=W3.rearrange("(m p) a -> p m a", p=P))
 
-        def h1_half(bh):
-            units = [
-                h1gp.tile([P, 2 * 512 * 4], BF16, name="h1g%d_%d" % (bh, gp), tag="h1g", align_bytes=64)
-                for gp in range(2)
-            ]
-            for ii in range(4):
-                words = h1raw[4 * bh + ii][:].bitcast(F32)
-                for gp in range(2):
-                    bank = psum.tile([P, 2, 2, P], F32, name="trb%d_%d_%d" % (bh, ii, gp), tag="bank")
-                    for gg in range(2):
-                        for u in range(2):
-                            w0 = 256 * (2 * gp + gg) + 128 * u
-                            nc.tensor.transpose(bank[:, gg, u, :], words[:, w0:w0 + P], ident[:])
-                    dst = units[gp][:].bitcast(F32).rearrange("p (g b u) -> p g b u", g=2, u=2)
-                    dst = dst[:, :, ii * P:(ii + 1) * P, :]
-                    src = bank[:].rearrange("p g u b -> p g b u")
-                    nc.scalar.copy(out=dst, in_=src)
-            for gp in range(2):
-                for gg in range(2):
-                    c = 2 * gp + gg
-                    nc.vector.quantize_mx(
-                        out=h1codes[:, c, 512 * bh:512 * bh + 512].bitcast(FP8X4),
-                        scales=h1sc[:, c, 512 * bh:512 * bh + 512],
-                        in_=units[gp][:, 2048 * gg:2048 * gg + 2048],
-                    )
+        ops = {}
+        st = {}
 
-        def w2_chunk(g, c):
-            src = w2raw[(g, c)]
-            grp = w2gp.tile([P, 512, 4], BF16, name="w2g%d_%d" % (g, c), tag="w2g", align_bytes=64)
-            nc.vector.tensor_copy(
-                out=grp[:, 0:WV, :].rearrange("p (c i) t -> p c t i", i=4),
-                in_=src[:, :, 0:WV].rearrange("p t (c i) -> p c t i", i=4),
-            )
-            nc.scalar.copy(
-                out=grp[:, WV:512, :].rearrange("p (c i) t -> p c t i", i=4),
-                in_=src[:, :, WV:512].rearrange("p t (c i) -> p c t i", i=4),
-            )
-            nc.vector.quantize_mx(
-                out=w2codes[:, c, 512 * g:512 * g + 512].bitcast(FP8X4),
-                scales=w2sc[:, c, 512 * g:512 * g + 512],
-                in_=grp[:].rearrange("p w t -> p (w t)"),
-            )
+        def bank(key, shape):
+            if key not in st:
+                st[key] = psum.tile(shape, F32, name="ps_" + key, tag="bank")
+            return st[key]
 
-        def mm1(g, bh, c_outer):
-            banks = [psum.tile([P, 512], F32, name="mm%d_%d_%d" % (g, bh, t), tag="bank") for t in range(4)]
-            if c_outer:
-                order = [(c, t) for c in range(4) for t in range(4)]
-            else:
-                order = [(c, t) for t in range(4) for c in range(4)]
-            for (c, t) in order:
-                m = 4 * g + t
-                nc.tensor.matmul_mx(
-                    out=banks[t][:],
-                    lhsT=w2codes[:, c, m * P:(m + 1) * P].bitcast(FP8X4),
-                    lhsT_scale=w2sc[:, c, m * P:(m + 1) * P],
-                    rhs=h1codes[:, c, 512 * bh:512 * bh + 512].bitcast(FP8X4),
-                    rhs_scale=h1sc[:, c, 512 * bh:512 * bh + 512],
-                    start=(c == 0),
-                    stop=(c == 3),
-                )
-            return banks
+        def big_tile(key, shape, dtype):
+            if key not in st:
+                st[key] = big.tile(shape, dtype, name="big_" + key, tag="big", align_bytes=64)
+            return st[key]
 
-        def epilogue(g, bh, banks):
-            a = apool.tile([P, 4, 512], F32, name="a%d_%d" % (g, bh), tag="a")
-            for t in range(4):
-                m = 4 * g + t
-                nc.scalar.activation(out=a[:, t, :], in_=banks[t][:], func=ACT.Identity,
-                                     bias=b2T[:, m:m + 1], scale=1.0)
-            h2g = h2gp.tile([P, 512, 4], BF16, name="h2g%d_%d" % (g, bh), tag="h2g", align_bytes=64)
-            av = a[:].rearrange("p t b -> p b t")
-            nc.vector.scalar_tensor_tensor(out=h2g[:], in0=av, scalar=SLOPE, in1=av,
-                                           op0=ALU.mult, op1=ALU.max)
-            nc.vector.quantize_mx(
-                out=h2codes[:, g, 512 * bh:512 * bh + 512].bitcast(FP8X4),
-                scales=h2sc[:, g, 512 * bh:512 * bh + 512],
-                in_=h2g[:].rearrange("p b t -> p (b t)"),
-            )
+        def f_b2c():
+            nc.vector.tensor_copy(out=b2rows32[:], in_=b2rows[:])
 
-        def head(j):
-            lg = lgp.tile([P, 4, A], F32, name="lg%d" % j, tag="lg")
-            for ii in range(4):
-                i = 4 * j + ii
-                for g in range(4):
-                    nc.tensor.matmul_mx(
-                        out=lg[:, ii, :],
-                        lhsT=h2codes[:, g, i * P:(i + 1) * P].bitcast(FP8X4),
-                        lhsT_scale=h2sc[:, g, i * P:(i + 1) * P],
-                        rhs=w3codes[:, g * A:(g + 1) * A].bitcast(FP8X4),
-                        rhs_scale=w3sc[:, g * A:(g + 1) * A],
-                        start=(g == 0),
-                        stop=(g == 3),
-                    )
-            nlp = sm.tile([P, 4, A], F32, name="nlp%d" % j, tag="nlp")
-            nc.vector.tensor_tensor(out=nlp[:], in0=nbm[:, 4 * j:4 * j + 4, :], in1=lg[:], op=ALU.subtract)
-            nmx = sm.tile([P, 4], F32, name="nmx%d" % j, tag="nmx")
-            nc.vector.tensor_reduce(out=nmx[:], in_=nlp[:], axis=AX.X, op=ALU.min)
-            e = sm.tile([P, 4, A], F32, name="e%d" % j, tag="e")
-            s = sm.tile([P, 4], F32, name="s%d" % j, tag="s")
-            for ii in range(4):
-                nc.scalar.activation(out=e[:, ii, :], in_=nlp[:, ii, :], func=ACT.Exp,
-                                     bias=nmx[:, ii:ii + 1], scale=-1.0, accum_out=s[:, ii:ii + 1])
-            r = sm.tile([P, 4], F32, name="r%d" % j, tag="r")
-            nc.vector.reciprocal(out=r[:], in_=s[:])
-            for ii in range(4):
-                nc.scalar.activation(out=e[:, ii, :], in_=e[:, ii, :], func=ACT.Copy, scale=r[:, ii:ii + 1])
-            nc.sync.dma_start(out=out[512 * j:512 * j + 512, :].rearrange("(i p) a -> p i a", p=P), in_=e[:])
+        def f_b2t():
+            cps = bank("cps", [P, 512])
+            nc.tensor.transpose(cps[:, 0:P], b2rows32[:], ident[:])
+            nc.tensor.matmul(out=cps[:, P:P + A], lhsT=ones[:], rhs=b3row[:], start=True, stop=True)
 
-        b2rows32 = const.tile([P, P], F32, name="b2rows32")
-        nc.vector.tensor_copy(out=b2rows32[:], in_=b2rows[:])
-        b2ps = psum.tile([P, 512], F32, name="b2ps", tag="bank")
-        nc.tensor.transpose(b2ps[:, 0:P], b2rows32[:], ident[:])
-        b2T = const.tile([P, 16], F32, name="b2T")
-        nc.vector.tensor_copy(out=b2T[:], in_=b2ps[:, 0:16])
+        def f_b2o():
+            cps = bank("cps", [P, 512])
+            nc.vector.tensor_copy(out=b2T[:], in_=cps[:, 0:16])
+            nc.vector.tensor_copy(out=b3bc[:], in_=cps[:, P:P + A])
 
-        nbm = const.tile([P, 8, A], F32, name="nbm")
-        for (i0, n, t) in xparts:
-            for i in range(n):
-                nc.vector.tensor_reduce(out=nbm[:, i0 + i, :],
-                                        in_=t[:, i, :].rearrange("p (a j) -> p a j", j=G),
+        ops["b2c"] = ((), f_b2c)
+        ops["b2t"] = (("b2c",), f_b2t)
+        ops["b2o"] = (("b2t",), f_b2o)
+
+        def mk_gs(i):
+            def f():
+                nc.vector.tensor_reduce(out=nbm[:, i, :], in_=xof[i].rearrange("p (a j) -> p a j", j=G),
                                         axis=AX.X, op=ALU.add)
-        nc.vector.tensor_scalar(out=nbm[:], in0=nbm[:], scalar1=0.0, scalar2=BIG,
-                                op0=ALU.is_equal, op1=ALU.mult)
-        nc.vector.tensor_tensor(out=nbm[:], in0=nbm[:],
-                                in1=b3bc[:].unsqueeze(1).to_broadcast([P, 8, A]), op=ALU.subtract)
+            return f
 
-        h1_half(0)
-        h1_half(1)
+        for i in range(8):
+            ops["gs%d" % i] = ((), mk_gs(i))
+
+        def f_mask2():
+            nc.vector.tensor_scalar(out=nbm[:], in0=nbm[:], scalar1=0.0, scalar2=BIG,
+                                    op0=ALU.is_equal, op1=ALU.mult)
+            nc.vector.tensor_tensor(out=nbm[:], in0=nbm[:],
+                                    in1=b3bc[:].unsqueeze(1).to_broadcast([P, 8, A]), op=ALU.subtract)
+
+        ops["mask2"] = (tuple(["gs%d" % i for i in range(8)] + ["b2o"]), f_mask2)
+
+        def mk_tr(i, gp):
+            def f():
+                words = h1raw[i][:].bitcast(F32)
+                bk = bank("tr%d_%d" % (i, gp), [P, 2, 2, P])
+                for gg in range(2):
+                    for u in range(2):
+                        w0 = 256 * (2 * gp + gg) + 128 * u
+                        nc.tensor.transpose(bk[:, gg, u, :], words[:, w0:w0 + P], ident[:])
+            return f
+
+        def mk_ho(i, gp):
+            def f():
+                bh, ii = i // 4, i % 4
+                unit = big_tile("h1g%d_%d" % (bh, gp), [P, 2 * 512 * 4], BF16)
+                dst = unit[:].bitcast(F32).rearrange("p (g b u) -> p g b u", g=2, u=2)
+                dst = dst[:, :, ii * P:(ii + 1) * P, :]
+                src = bank("tr%d_%d" % (i, gp), [P, 2, 2, P])[:].rearrange("p g u b -> p g b u")
+                nc.scalar.copy(out=dst, in_=src)
+            return f
+
+        def mk_h1q(bh, c):
+            def f():
+                unit = big_tile("h1g%d_%d" % (bh, c // 2), [P, 2 * 512 * 4], BF16)
+                nc.vector.quantize_mx(
+                    out=h1codes[:, c, 512 * bh:512 * bh + 512].bitcast(FP8X4),
+                    scales=h1sc[:, c, 512 * bh:512 * bh + 512],
+                    in_=unit[:, 2048 * (c % 2):2048 * (c % 2) + 2048],
+                )
+            return f
+
+        for i in range(8):
+            for gp in range(2):
+                ops["tr%d.%d" % (i, gp)] = ((), mk_tr(i, gp))
+                ops["ho%d.%d" % (i, gp)] = (("tr%d.%d" % (i, gp),), mk_ho(i, gp))
+        for bh in range(2):
+            for c in range(4):
+                ops["h1q%d.%d" % (bh, c)] = (tuple(["ho%d.%d" % (4 * bh + ii, c // 2) for ii in range(4)]),
+                                             mk_h1q(bh, c))
+
+        def w2g_tile(k):
+            key = "w2g%d" % k
+            if key not in st:
+                st[key] = w2gp.tile([P, 512, 4], BF16, name=key, tag="w2g", align_bytes=64)
+            return st[key]
+
+        def regroup(copy, k, lo, hi):
+            copy(out=w2g_tile(k)[:, lo:hi, :].rearrange("p (c i) t -> p c t i", i=4),
+                 in_=w2raw[k][:, :, lo:hi].rearrange("p t (c i) -> p c t i", i=4))
+
+        def mk_rv(k):
+            return lambda: regroup(nc.vector.tensor_copy, k, 0, WVS[k // 4])
+
+        def mk_rs(k, z):
+            wv = WVS[k // 4]
+            half = (512 - wv) // 2
+            return lambda: regroup(nc.scalar.copy, k, wv + z * half, wv + (z + 1) * half)
+
+        def mk_qw(k):
+            def f():
+                g, c = k // 4, k % 4
+                nc.vector.quantize_mx(
+                    out=w2codes[:, c, 512 * g:512 * g + 512].bitcast(FP8X4),
+                    scales=w2sc[:, c, 512 * g:512 * g + 512],
+                    in_=w2g_tile(k)[:].rearrange("p w t -> p (w t)"),
+                )
+            return f
+
+        for k in range(16):
+            ops["rV%d" % k] = ((), mk_rv(k))
+            ops["rS%d.0" % k] = ((), mk_rs(k, 0))
+            ops["rS%d.1" % k] = ((), mk_rs(k, 1))
+            ops["qW%d" % k] = (("rV%d" % k, "rS%d.0" % k, "rS%d.1" % k), mk_qw(k))
+
+        def mx1(dst, m, c, b0, n):
+            nc.tensor.matmul_mx(
+                out=dst,
+                lhsT=w2codes[:, c, m * P:(m + 1) * P].bitcast(FP8X4),
+                lhsT_scale=w2sc[:, c, m * P:(m + 1) * P],
+                rhs=h1codes[:, c, b0:b0 + n].bitcast(FP8X4),
+                rhs_scale=h1sc[:, c, b0:b0 + n],
+                start=(c == 0),
+                stop=(c == 3),
+            )
+
+        def group_ap(u, t):
+            g, i0, nb = UNITS[u]
+            if nb == 4:
+                return bank("g%d_%d" % (u, t), [P, 512])[:]
+            return bank("g%d_%d" % (u, t // 2), [P, 2, 256])[:, t % 2, :]
+
+        def mk_p0(c):
+            def f():
+                for u in range(2):
+                    for t in range(4):
+                        mx1(group_ap(u, t), t, c, 512 * u, 512)
+            return f
 
         for c in range(4):
-            w2_chunk(0, c)
-        for g in range(4):
-            banks0 = mm1(g, 0, g == 0)
-            if g < 3:
-                w2_chunk(g + 1, 0)
-                w2_chunk(g + 1, 1)
-            epilogue(g, 0, banks0)
-            banks1 = mm1(g, 1, False)
-            if g < 3:
-                w2_chunk(g + 1, 2)
-                w2_chunk(g + 1, 3)
-            if g == 2:
-                w3g = const.tile([P, 4, A, 4], BF16, name="w3g", align_bytes=64)
-                nc.vector.tensor_copy(out=w3g[:], in_=w3raw[:].rearrange("p (g t) a -> p g a t", t=4))
-                nc.vector.quantize_mx(out=w3codes[:].bitcast(FP8X4), scales=w3sc[:],
-                                      in_=w3g[:].rearrange("p g a t -> p (g a t)"))
-            epilogue(g, 1, banks1)
-            if g == 3:
-                head(0)
-        head(1)
+            deps = ["qW%d" % c, "h1q0.%d" % c, "h1q1.%d" % c]
+            if c > 0:
+                deps.append("p0.%d" % (c - 1))
+            ops["p0.%d" % c] = (tuple(deps), mk_p0(c))
+
+        def mk_grp(u, t):
+            def f():
+                g, i0, nb = UNITS[u]
+                for c in range(4):
+                    mx1(group_ap(u, t), 4 * g + t, c, P * i0, P * nb)
+            return f
+
+        def mk_bias(u, t):
+            def f():
+                g, i0, nb = UNITS[u]
+                a = big_tile("a%d" % u, [P, 4, P * nb], F32)
+                nc.scalar.activation(out=a[:, t, :], in_=group_ap(u, t), func=ACT.Identity,
+                                     bias=b2T[:, 4 * g + t:4 * g + t + 1], scale=1.0)
+            return f
+
+        def mk_leaky(u):
+            def f():
+                g, i0, nb = UNITS[u]
+                a = big_tile("a%d" % u, [P, 4, P * nb], F32)
+                st["h2g%d" % u] = h2gp.tile([P, P * nb, 4], BF16, name="h2g%d" % u, tag="h2g", align_bytes=64)
+                av = a[:].rearrange("p t b -> p b t")
+                nc.vector.scalar_tensor_tensor(out=st["h2g%d" % u][:], in0=av, scalar=SLOPE, in1=av,
+                                               op0=ALU.mult, op1=ALU.max)
+            return f
+
+        def mk_qh(u):
+            def f():
+                g, i0, nb = UNITS[u]
+                nc.vector.quantize_mx(
+                    out=h2codes[:, g, P * i0:P * (i0 + nb)].bitcast(FP8X4),
+                    scales=h2sc[:, g, P * i0:P * (i0 + nb)],
+                    in_=st["h2g%d" % u][:].rearrange("p b t -> p (b t)"),
+                )
+            return f
+
+        for u in range(len(UNITS)):
+            g, i0, nb = UNITS[u]
+            for t in range(4):
+                if g > 0:
+                    ops["G%d.%d" % (u, t)] = (tuple(["qW%d" % (4 * g + c) for c in range(4)]
+                                                    + ["h1q%d.%d" % (i0 // 4, c) for c in range(4)]), mk_grp(u, t))
+                    ops["bi%d.%d" % (u, t)] = (("G%d.%d" % (u, t), "b2o"), mk_bias(u, t))
+                else:
+                    ops["bi%d.%d" % (u, t)] = (("p0.3", "b2o"), mk_bias(u, t))
+            ops["st%d" % u] = (tuple(["bi%d.%d" % (u, t) for t in range(4)]), mk_leaky(u))
+            ops["qH%d" % u] = (("st%d" % u,), mk_qh(u))
+
+        def f_w3r():
+            nc.vector.tensor_copy(out=w3g[:], in_=w3raw[:].rearrange("p (g t) a -> p g a t", t=4))
+
+        def f_w3q():
+            nc.vector.quantize_mx(out=w3codes[:].bitcast(FP8X4), scales=w3sc[:],
+                                  in_=w3g[:].rearrange("p g a t -> p (g a t)"))
+
+        ops["w3r"] = ((), f_w3r)
+        ops["w3q"] = (("w3r",), f_w3q)
+
+        def mk_m2(h):
+            def f():
+                lg = bank("lg%d" % h, [P, 2, A])
+                for ii in range(2):
+                    i = 2 * h + ii
+                    for g in range(4):
+                        nc.tensor.matmul_mx(
+                            out=lg[:, ii, :],
+                            lhsT=h2codes[:, g, i * P:(i + 1) * P].bitcast(FP8X4),
+                            lhsT_scale=h2sc[:, g, i * P:(i + 1) * P],
+                            rhs=w3codes[:, g * A:(g + 1) * A].bitcast(FP8X4),
+                            rhs_scale=w3sc[:, g * A:(g + 1) * A],
+                            start=(g == 0),
+                            stop=(g == 3),
+                        )
+            return f
+
+        def mk_nl(h):
+            def f():
+                st["nlp%d" % h] = sm.tile([P, 2, A], F32, name="nlp%d" % h, tag="nlp")
+                nc.vector.tensor_tensor(out=st["nlp%d" % h][:], in0=nbm[:, 2 * h:2 * h + 2, :],
+                                        in1=bank("lg%d" % h, [P, 2, A])[:], op=ALU.subtract)
+            return f
+
+        def mk_mn(h):
+            def f():
+                st["nmx%d" % h] = sm.tile([P, 2], F32, name="nmx%d" % h, tag="nmx")
+                nc.vector.tensor_reduce(out=st["nmx%d" % h][:], in_=st["nlp%d" % h][:], axis=AX.X, op=ALU.min)
+            return f
+
+        def mk_ex(h):
+            def f():
+                st["e%d" % h] = sm.tile([P, 2, A], F32, name="e%d" % h, tag="e")
+                st["s%d" % h] = sm.tile([P, 2], F32, name="s%d" % h, tag="s")
+                for ii in range(2):
+                    nc.scalar.activation(out=st["e%d" % h][:, ii, :], in_=st["nlp%d" % h][:, ii, :], func=ACT.Exp,
+                                         bias=st["nmx%d" % h][:, ii:ii + 1], scale=-1.0,
+                                         accum_out=st["s%d" % h][:, ii:ii + 1])
+            return f
+
+        def mk_rc(h):
+            def f():
+                st["r%d" % h] = sm.tile([P, 2], F32, name="r%d" % h, tag="r")
+                nc.vector.reciprocal(out=st["r%d" % h][:], in_=st["s%d" % h][:])
+            return f
+
+        def mk_sc(h):
+            def f():
+                e = st["e%d" % h]
+                for ii in range(2):
+                    nc.scalar.activation(out=e[:, ii, :], in_=e[:, ii, :], func=ACT.Copy,
+                                         scale=st["r%d" % h][:, ii:ii + 1])
+                nc.sync.dma_start(out=out[256 * h:256 * h + 256, :].rearrange("(i p) a -> p i a", p=P), in_=e[:])
+            return f
+
+        for h in range(4):
+            deps = ["w3q"]
+            for u in range(len(UNITS)):
+                g, i0, nb = UNITS[u]
+                if i0 < 2 * h + 2 and 2 * h < i0 + nb:
+                    deps.append("qH%d" % u)
+            ops["m2.%d" % h] = (tuple(deps), mk_m2(h))
+            ops["nl%d" % h] = (("m2.%d" % h, "mask2"), mk_nl(h))
+            ops["mn%d" % h] = (("nl%d" % h,), mk_mn(h))
+            ops["ex%d" % h] = (("mn%d" % h,), mk_ex(h))
+            ops["rc%d" % h] = (("ex%d" % h,), mk_rc(h))
+            ops["sc%d" % h] = (("rc%d" % h,), mk_sc(h))
+
+        te = ["b2t"]
+        sc = []
+        ve = ["b2c", "b2o"] + ["gs%d" % i for i in range(8)] + ["mask2"]
+        for i in range(8):
+            for gp in range(2):
+                te.append("tr%d.%d" % (i, gp))
+                sc.append("ho%d.%d" % (i, gp))
+        ve += ["h1q%d.%d" % (bh, c) for bh in range(2) for c in range(4)]
+        te += ["p0.%d" % c for c in range(4)]
+        pieces = ["rS%d.%d" % (k, z) for k in range(16) for z in range(2)]
+        biases = ["bi%d.%d" % (u, t) for u in range(6) for t in range(4)]
+        sc += pieces[:AHEAD]
+        rest = pieces[AHEAD:]
+        for j in range(len(biases)):
+            sc.append(biases[j])
+            if j < len(rest):
+                sc.append(rest[j])
+        late = []
+        for u in range(6):
+            late += ["st%d" % u, "qH%d" % u]
+        for k in range(17):
+            if k < 16:
+                ve.append("rV%d" % k)
+            if k >= EFROM:
+                ve.append(late.pop(0))
+            if k == 13:
+                ve.append("w3r")
+            if k >= 1:
+                ve.append("qW%d" % (k - 1))
+            if k == 14:
+                ve.append("w3q")
+        ve += late
+        te += ["G%d.%d" % (u, t) for u in range(2, 9) for t in range(4)]
+        te += ["m2.0"] + ["G9.%d" % t for t in range(4)] + ["m2.1", "m2.2", "m2.3"]
+        sc += ["bi%d.%d" % (u, t) for u in range(6, 9) for t in range(4)]
+        sc += ["ex0"] + ["bi9.%d" % t for t in range(4)] + ["sc0", "ex1", "sc1", "ex2", "sc2", "ex3", "sc3"]
+        ve += ["st6", "qH6", "st7", "qH7", "nl0", "mn0", "st8", "qH8", "rc0", "nl1", "mn1",
+               "st9", "qH9", "rc1", "nl2", "mn2", "nl3", "mn3", "rc2", "rc3"]
+
+        queues = [te, sc, ve]
+        assert sum([len(q) for q in queues]) == len(ops)
+        pos = [0, 0, 0]
+        done = set()
+        moved = True
+        while moved:
+            moved = False
+            for qi in range(3):
+                while pos[qi] < len(queues[qi]) and all([d in done for d in ops[queues[qi][pos[qi]]][0]]):
+                    key = queues[qi][pos[qi]]
+                    ops[key][1]()
+                    done.add(key)
+                    pos[qi] += 1
+                    moved = True
+        assert len(done) == len(ops)

@@ -18,7 +18,7 @@ SLOPE = 0.4
 BIG = 1.0e30
 FLOPS = 2 * B * H1 * H2 + 2 * B * H2 * A
 
-PIN = False
+PIN = True
 WVS = (128, 416, 256, 160)
 AHEAD = 14
 EFROM = 9

@@ -18,11 +18,10 @@ SLOPE = 0.4
 BIG = 1.0e30
 FLOPS = 2 * B * H1 * H2 + 2 * B * H2 * A
 
-PIN = True
-WVS = (128, 416, 256, 160)
-AHEAD = 14
-EFROM = 9
+WVS = (320, 224, 224, 160)
+LAG = 1
 UNITS = [(0, 0, 4), (0, 4, 4), (1, 0, 4), (1, 4, 4), (2, 0, 4), (2, 4, 4), (3, 0, 2), (3, 2, 2), (3, 4, 2), (3, 6, 2)]
+HEAD = 2
 
 
 def tile_dqn_pa_kernel(tc, x, h1, W2, b2, W3, b3, out):
@@ -35,8 +34,6 @@ def tile_dqn_pa_kernel(tc, x, h1, W2, b2, W3, b3, out):
         h2gp = ctx.enter_context(tc.tile_pool(name="h2gp", bufs=2))
         sm = ctx.enter_context(tc.tile_pool(name="sm", bufs=2))
         psum = ctx.enter_context(tc.psum_pool(name="psum", bufs=8))
-        if PIN:
-            ctx.enter_context(tc.manual_schedule())
 
         ident = const.tile([P, P], F32, name="ident")
         make_identity(nc, ident[:])
@@ -48,7 +45,6 @@ def tile_dqn_pa_kernel(tc, x, h1, W2, b2, W3, b3, out):
         nc.scalar.dma_start(out=b2rows[0:16, :], in_=b2.rearrange("(m p) -> m p", p=P))
         b3row = const.tile([P, A], BF16, name="b3row")
         nc.vector.memset(b3row[:], 0.0)
-        nc.scalar.dma_start(out=b3row[0:1, :], in_=b3.rearrange("(o a) -> o a", o=1))
         ones = const.tile([P, P], BF16, name="ones")
         nc.vector.memset(ones[:], 1.0)
 
@@ -60,23 +56,31 @@ def tile_dqn_pa_kernel(tc, x, h1, W2, b2, W3, b3, out):
         h2sc = const.tile([P, 4, B], U8, name="h2sc", align_bytes=64)
         w3codes = const.tile([P, 4 * A], U32, name="w3codes", align_bytes=64)
         w3sc = const.tile([P, 4 * A], U8, name="w3sc", align_bytes=64)
-        b2rows32 = const.tile([P, P], F32, name="b2rows32")
-        b2T = const.tile([P, 16], F32, name="b2T")
-        b3bc = const.tile([P, A], F32, name="b3bc")
-        nbm = const.tile([P, 8, A], F32, name="nbm")
-        w3g = const.tile([P, 4, A, 4], BF16, name="w3g", align_bytes=64)
 
-        xof = {}
-        for (i0, n) in ((0, 3), (3, 3), (6, 2)):
+        xparts = []
+        h1raw = []
+
+        def load_x(i0, n):
             t = raw.tile([P, n, A * G], BF16, name="xraw%d" % i0, tag="raw")
             nc.sync.dma_start(out=t[:], in_=x[i0 * P:(i0 + n) * P, :].rearrange("(i p) c -> p i c", p=P))
-            for i in range(n):
-                xof[i0 + i] = t[:, i, :]
-        h1raw = []
-        for i in range(8):
+            xparts.append((i0, n, t))
+
+        def load_h1(i):
             t = raw.tile([P, H1], BF16, name="h1raw%d" % i, tag="raw")
             nc.sync.dma_start(out=t[:], in_=h1[i * P:(i + 1) * P, :])
             h1raw.append(t)
+
+        load_h1(0)
+        load_x(0, 3)
+        load_h1(1)
+        load_h1(2)
+        load_x(3, 3)
+        load_h1(3)
+        load_h1(4)
+        load_x(6, 2)
+        for i in range(5, 8):
+            load_h1(i)
+        nc.sync.dma_start(out=b3row[0:1, :], in_=b3.rearrange("(o a) -> o a", o=1))
         w2raw = []
         for k in range(16):
             g, c = k // 4, k % 4
@@ -91,332 +95,170 @@ def tile_dqn_pa_kernel(tc, x, h1, W2, b2, W3, b3, out):
         w3raw = raw.tile([P, 16, A], BF16, name="w3raw", tag="raw")
         nc.sync.dma_start(out=w3raw[:], in_=W3.rearrange("(m p) a -> p m a", p=P))
 
-        ops = {}
-        st = {}
-
-        def bank(key, shape):
-            if key not in st:
-                st[key] = psum.tile(shape, F32, name="ps_" + key, tag="bank")
-            return st[key]
-
-        def big_tile(key, shape, dtype):
-            if key not in st:
-                st[key] = big.tile(shape, dtype, name="big_" + key, tag="big", align_bytes=64)
-            return st[key]
-
-        def f_b2c():
-            nc.vector.tensor_copy(out=b2rows32[:], in_=b2rows[:])
-
-        def f_b2t():
-            cps = bank("cps", [P, 512])
-            nc.tensor.transpose(cps[:, 0:P], b2rows32[:], ident[:])
-            nc.tensor.matmul(out=cps[:, P:P + A], lhsT=ones[:], rhs=b3row[:], start=True, stop=True)
-
-        def f_b2o():
-            cps = bank("cps", [P, 512])
-            nc.vector.tensor_copy(out=b2T[:], in_=cps[:, 0:16])
-            nc.vector.tensor_copy(out=b3bc[:], in_=cps[:, P:P + A])
-
-        ops["b2c"] = ((), f_b2c)
-        ops["b2t"] = (("b2c",), f_b2t)
-        ops["b2o"] = (("b2t",), f_b2o)
-
-        def mk_gs(i):
-            def f():
-                nc.vector.tensor_reduce(out=nbm[:, i, :], in_=xof[i].rearrange("p (a j) -> p a j", j=G),
-                                        axis=AX.X, op=ALU.add)
-            return f
-
-        for i in range(8):
-            ops["gs%d" % i] = ((), mk_gs(i))
-
-        def f_mask2():
-            nc.vector.tensor_scalar(out=nbm[:], in0=nbm[:], scalar1=0.0, scalar2=BIG,
-                                    op0=ALU.is_equal, op1=ALU.mult)
-            nc.vector.tensor_tensor(out=nbm[:], in0=nbm[:],
-                                    in1=b3bc[:].unsqueeze(1).to_broadcast([P, 8, A]), op=ALU.subtract)
-
-        ops["mask2"] = (tuple(["gs%d" % i for i in range(8)] + ["b2o"]), f_mask2)
-
-        def mk_tr(i, gp):
-            def f():
-                words = h1raw[i][:].bitcast(F32)
-                bk = bank("tr%d_%d" % (i, gp), [P, 2, 2, P])
-                for gg in range(2):
-                    for u in range(2):
-                        w0 = 256 * (2 * gp + gg) + 128 * u
-                        nc.tensor.transpose(bk[:, gg, u, :], words[:, w0:w0 + P], ident[:])
-            return f
-
-        def mk_ho(i, gp):
-            def f():
-                bh, ii = i // 4, i % 4
-                unit = big_tile("h1g%d_%d" % (bh, gp), [P, 2 * 512 * 4], BF16)
-                dst = unit[:].bitcast(F32).rearrange("p (g b u) -> p g b u", g=2, u=2)
-                dst = dst[:, :, ii * P:(ii + 1) * P, :]
-                src = bank("tr%d_%d" % (i, gp), [P, 2, 2, P])[:].rearrange("p g u b -> p g b u")
-                nc.scalar.copy(out=dst, in_=src)
-            return f
-
-        def mk_h1q(bh, c):
-            def f():
-                unit = big_tile("h1g%d_%d" % (bh, c // 2), [P, 2 * 512 * 4], BF16)
+        def h1_half(bh):
+            units = [
+                big.tile([P, 2 * 512 * 4], BF16, name="h1g%d_%d" % (bh, gp), tag="big", align_bytes=64)
+                for gp in range(2)
+            ]
+            for ii in range(4):
+                words = h1raw[4 * bh + ii][:].bitcast(F32)
+                for gp in range(2):
+                    bank = psum.tile([P, 2, 2, P], F32, name="trb%d_%d_%d" % (bh, ii, gp), tag="bank")
+                    for gg in range(2):
+                        for u in range(2):
+                            w0 = 256 * (2 * gp + gg) + 128 * u
+                            nc.tensor.transpose(bank[:, gg, u, :], words[:, w0:w0 + P], ident[:])
+                    dst = units[gp][:].bitcast(F32).rearrange("p (g b u) -> p g b u", g=2, u=2)
+                    dst = dst[:, :, ii * P:(ii + 1) * P, :]
+                    nc.scalar.copy(out=dst, in_=bank[:].rearrange("p g u b -> p g b u"))
+            for c in range(4):
                 nc.vector.quantize_mx(
                     out=h1codes[:, c, 512 * bh:512 * bh + 512].bitcast(FP8X4),
                     scales=h1sc[:, c, 512 * bh:512 * bh + 512],
-                    in_=unit[:, 2048 * (c % 2):2048 * (c % 2) + 2048],
+                    in_=units[c // 2][:, 2048 * (c % 2):2048 * (c % 2) + 2048],
                 )
-            return f
 
-        for i in range(8):
-            for gp in range(2):
-                ops["tr%d.%d" % (i, gp)] = ((), mk_tr(i, gp))
-                ops["ho%d.%d" % (i, gp)] = (("tr%d.%d" % (i, gp),), mk_ho(i, gp))
-        for bh in range(2):
-            for c in range(4):
-                ops["h1q%d.%d" % (bh, c)] = (tuple(["ho%d.%d" % (4 * bh + ii, c // 2) for ii in range(4)]),
-                                             mk_h1q(bh, c))
-
-        def w2g_tile(k):
-            key = "w2g%d" % k
-            if key not in st:
-                st[key] = w2gp.tile([P, 512, 4], BF16, name=key, tag="w2g", align_bytes=64)
-            return st[key]
-
-        def regroup(copy, k, lo, hi):
-            copy(out=w2g_tile(k)[:, lo:hi, :].rearrange("p (c i) t -> p c t i", i=4),
-                 in_=w2raw[k][:, :, lo:hi].rearrange("p t (c i) -> p c t i", i=4))
-
-        def mk_rv(k):
-            return lambda: regroup(nc.vector.tensor_copy, k, 0, WVS[k // 4])
-
-        def mk_rs(k, z):
-            wv = WVS[k // 4]
-            half = (512 - wv) // 2
-            return lambda: regroup(nc.scalar.copy, k, wv + z * half, wv + (z + 1) * half)
-
-        def mk_qw(k):
-            def f():
-                g, c = k // 4, k % 4
-                nc.vector.quantize_mx(
-                    out=w2codes[:, c, 512 * g:512 * g + 512].bitcast(FP8X4),
-                    scales=w2sc[:, c, 512 * g:512 * g + 512],
-                    in_=w2g_tile(k)[:].rearrange("p w t -> p (w t)"),
-                )
-            return f
-
-        for k in range(16):
-            ops["rV%d" % k] = ((), mk_rv(k))
-            ops["rS%d.0" % k] = ((), mk_rs(k, 0))
-            ops["rS%d.1" % k] = ((), mk_rs(k, 1))
-            ops["qW%d" % k] = (("rV%d" % k, "rS%d.0" % k, "rS%d.1" % k), mk_qw(k))
-
-        def mx1(dst, m, c, b0, n):
-            nc.tensor.matmul_mx(
-                out=dst,
-                lhsT=w2codes[:, c, m * P:(m + 1) * P].bitcast(FP8X4),
-                lhsT_scale=w2sc[:, c, m * P:(m + 1) * P],
-                rhs=h1codes[:, c, b0:b0 + n].bitcast(FP8X4),
-                rhs_scale=h1sc[:, c, b0:b0 + n],
-                start=(c == 0),
-                stop=(c == 3),
+        def w2_chunk(k):
+            g, c = k // 4, k % 4
+            wv = WVS[g]
+            src = w2raw[k]
+            grp = w2gp.tile([P, 512, 4], BF16, name="w2g%d" % k, tag="w2g", align_bytes=64)
+            nc.vector.tensor_copy(
+                out=grp[:, 0:wv, :].rearrange("p (c i) t -> p c t i", i=4),
+                in_=src[:, :, 0:wv].rearrange("p t (c i) -> p c t i", i=4),
+            )
+            nc.scalar.copy(
+                out=grp[:, wv:512, :].rearrange("p (c i) t -> p c t i", i=4),
+                in_=src[:, :, wv:512].rearrange("p t (c i) -> p c t i", i=4),
+            )
+            nc.vector.quantize_mx(
+                out=w2codes[:, c, 512 * g:512 * g + 512].bitcast(FP8X4),
+                scales=w2sc[:, c, 512 * g:512 * g + 512],
+                in_=grp[:].rearrange("p w t -> p (w t)"),
             )
 
-        def group_ap(u, t):
+        def mm1(u, c_outer):
             g, i0, nb = UNITS[u]
-            if nb == 4:
-                return bank("g%d_%d" % (u, t), [P, 512])[:]
-            return bank("g%d_%d" % (u, t // 2), [P, 2, 256])[:, t % 2, :]
-
-        def mk_p0(c):
-            def f():
-                for u in range(2):
-                    for t in range(4):
-                        mx1(group_ap(u, t), t, c, 512 * u, 512)
-            return f
-
-        for c in range(4):
-            deps = ["qW%d" % c, "h1q0.%d" % c, "h1q1.%d" % c]
-            if c > 0:
-                deps.append("p0.%d" % (c - 1))
-            ops["p0.%d" % c] = (tuple(deps), mk_p0(c))
-
-        def mk_grp(u, t):
-            def f():
-                g, i0, nb = UNITS[u]
-                for c in range(4):
-                    mx1(group_ap(u, t), 4 * g + t, c, P * i0, P * nb)
-            return f
-
-        def mk_bias(u, t):
-            def f():
-                g, i0, nb = UNITS[u]
-                a = big_tile("a%d" % u, [P, 4, P * nb], F32)
-                nc.scalar.activation(out=a[:, t, :], in_=group_ap(u, t), func=ACT.Identity,
-                                     bias=b2T[:, 4 * g + t:4 * g + t + 1], scale=1.0)
-            return f
-
-        def mk_leaky(u):
-            def f():
-                g, i0, nb = UNITS[u]
-                a = big_tile("a%d" % u, [P, 4, P * nb], F32)
-                st["h2g%d" % u] = h2gp.tile([P, P * nb, 4], BF16, name="h2g%d" % u, tag="h2g", align_bytes=64)
-                av = a[:].rearrange("p t b -> p b t")
-                nc.vector.scalar_tensor_tensor(out=st["h2g%d" % u][:], in0=av, scalar=SLOPE, in1=av,
-                                               op0=ALU.mult, op1=ALU.max)
-            return f
-
-        def mk_qh(u):
-            def f():
-                g, i0, nb = UNITS[u]
-                nc.vector.quantize_mx(
-                    out=h2codes[:, g, P * i0:P * (i0 + nb)].bitcast(FP8X4),
-                    scales=h2sc[:, g, P * i0:P * (i0 + nb)],
-                    in_=st["h2g%d" % u][:].rearrange("p b t -> p (b t)"),
+            n = P * nb
+            per = 512 // n
+            banks = [psum.tile([P, per, n], F32, name="mm%d_%d" % (u, j), tag="bank") for j in range(4 // per)]
+            groups = [banks[t // per][:, t % per, :] for t in range(4)]
+            if c_outer:
+                order = [(c, t) for c in range(4) for t in range(4)]
+            else:
+                order = [(c, t) for t in range(4) for c in range(4)]
+            for (c, t) in order:
+                m = 4 * g + t
+                nc.tensor.matmul_mx(
+                    out=groups[t],
+                    lhsT=w2codes[:, c, m * P:(m + 1) * P].bitcast(FP8X4),
+                    lhsT_scale=w2sc[:, c, m * P:(m + 1) * P],
+                    rhs=h1codes[:, c, P * i0:P * i0 + n].bitcast(FP8X4),
+                    rhs_scale=h1sc[:, c, P * i0:P * i0 + n],
+                    start=(c == 0),
+                    stop=(c == 3),
                 )
-            return f
+            return groups
 
-        for u in range(len(UNITS)):
+        def epilogue(u, groups):
             g, i0, nb = UNITS[u]
+            n = P * nb
+            a = big.tile([P, 4, n], F32, name="a%d" % u, tag="big", align_bytes=64)
             for t in range(4):
-                if g > 0:
-                    ops["G%d.%d" % (u, t)] = (tuple(["qW%d" % (4 * g + c) for c in range(4)]
-                                                    + ["h1q%d.%d" % (i0 // 4, c) for c in range(4)]), mk_grp(u, t))
-                    ops["bi%d.%d" % (u, t)] = (("G%d.%d" % (u, t), "b2o"), mk_bias(u, t))
-                else:
-                    ops["bi%d.%d" % (u, t)] = (("p0.3", "b2o"), mk_bias(u, t))
-            ops["st%d" % u] = (tuple(["bi%d.%d" % (u, t) for t in range(4)]), mk_leaky(u))
-            ops["qH%d" % u] = (("st%d" % u,), mk_qh(u))
+                m = 4 * g + t
+                nc.scalar.activation(out=a[:, t, :], in_=groups[t], func=ACT.Identity,
+                                     bias=b2T[:, m:m + 1], scale=1.0)
+            h2g = h2gp.tile([P, n, 4], BF16, name="h2g%d" % u, tag="h2g", align_bytes=64)
+            av = a[:].rearrange("p t b -> p b t")
+            nc.vector.scalar_tensor_tensor(out=h2g[:], in0=av, scalar=SLOPE, in1=av,
+                                           op0=ALU.mult, op1=ALU.max)
+            nc.vector.quantize_mx(
+                out=h2codes[:, g, P * i0:P * i0 + n].bitcast(FP8X4),
+                scales=h2sc[:, g, P * i0:P * i0 + n],
+                in_=h2g[:].rearrange("p b t -> p (b t)"),
+            )
 
-        def f_w3r():
-            nc.vector.tensor_copy(out=w3g[:], in_=w3raw[:].rearrange("p (g t) a -> p g a t", t=4))
+        def head(j):
+            lg = psum.tile([P, HEAD, A], F32, name="lg%d" % j, tag="bank")
+            for ii in range(HEAD):
+                i = HEAD * j + ii
+                for g in range(4):
+                    nc.tensor.matmul_mx(
+                        out=lg[:, ii, :],
+                        lhsT=h2codes[:, g, i * P:(i + 1) * P].bitcast(FP8X4),
+                        lhsT_scale=h2sc[:, g, i * P:(i + 1) * P],
+                        rhs=w3codes[:, g * A:(g + 1) * A].bitcast(FP8X4),
+                        rhs_scale=w3sc[:, g * A:(g + 1) * A],
+                        start=(g == 0),
+                        stop=(g == 3),
+                    )
+            nlp = sm.tile([P, HEAD, A], F32, name="nlp%d" % j, tag="nlp")
+            nc.vector.tensor_tensor(out=nlp[:], in0=nbm[:, HEAD * j:HEAD * (j + 1), :], in1=lg[:], op=ALU.subtract)
+            nmx = sm.tile([P, HEAD], F32, name="nmx%d" % j, tag="nmx")
+            nc.vector.tensor_reduce(out=nmx[:], in_=nlp[:], axis=AX.X, op=ALU.min)
+            e = sm.tile([P, HEAD, A], F32, name="e%d" % j, tag="e")
+            s = sm.tile([P, HEAD], F32, name="s%d" % j, tag="s")
+            for ii in range(HEAD):
+                nc.scalar.activation(out=e[:, ii, :], in_=nlp[:, ii, :], func=ACT.Exp,
+                                     bias=nmx[:, ii:ii + 1], scale=-1.0, accum_out=s[:, ii:ii + 1])
+            r = sm.tile([P, HEAD], F32, name="r%d" % j, tag="r")
+            nc.vector.reciprocal(out=r[:], in_=s[:])
+            for ii in range(HEAD):
+                nc.scalar.activation(out=e[:, ii, :], in_=e[:, ii, :], func=ACT.Copy, scale=r[:, ii:ii + 1])
+            rows = P * HEAD
+            nc.sync.dma_start(out=out[rows * j:rows * (j + 1), :].rearrange("(i p) a -> p i a", p=P), in_=e[:])
 
-        def f_w3q():
-            nc.vector.quantize_mx(out=w3codes[:].bitcast(FP8X4), scales=w3sc[:],
-                                  in_=w3g[:].rearrange("p g a t -> p (g a t)"))
+        nbm = const.tile([P, 8, A], F32, name="nbm")
+        for (i0, n, t) in xparts:
+            for i in range(n):
+                nc.vector.tensor_reduce(out=nbm[:, i0 + i, :],
+                                        in_=t[:, i, :].rearrange("p (a j) -> p a j", j=G),
+                                        axis=AX.X, op=ALU.add)
+        nc.vector.tensor_scalar(out=nbm[:], in0=nbm[:], scalar1=0.0, scalar2=BIG,
+                                op0=ALU.is_equal, op1=ALU.mult)
 
-        ops["w3r"] = ((), f_w3r)
-        ops["w3q"] = (("w3r",), f_w3q)
+        h1_half(0)
+        h1_half(1)
 
-        def mk_m2(h):
-            def f():
-                lg = bank("lg%d" % h, [P, 2, A])
-                for ii in range(2):
-                    i = 2 * h + ii
-                    for g in range(4):
-                        nc.tensor.matmul_mx(
-                            out=lg[:, ii, :],
-                            lhsT=h2codes[:, g, i * P:(i + 1) * P].bitcast(FP8X4),
-                            lhsT_scale=h2sc[:, g, i * P:(i + 1) * P],
-                            rhs=w3codes[:, g * A:(g + 1) * A].bitcast(FP8X4),
-                            rhs_scale=w3sc[:, g * A:(g + 1) * A],
-                            start=(g == 0),
-                            stop=(g == 3),
-                        )
-            return f
+        b2rows32 = const.tile([P, P], F32, name="b2rows32")
+        nc.vector.tensor_copy(out=b2rows32[:], in_=b2rows[:])
+        b2ps = psum.tile([P, 512], F32, name="b2ps", tag="bank")
+        nc.tensor.transpose(b2ps[:, 0:P], b2rows32[:], ident[:])
+        b2T = const.tile([P, 16], F32, name="b2T")
+        nc.vector.tensor_copy(out=b2T[:], in_=b2ps[:, 0:16])
 
-        def mk_nl(h):
-            def f():
-                st["nlp%d" % h] = sm.tile([P, 2, A], F32, name="nlp%d" % h, tag="nlp")
-                nc.vector.tensor_tensor(out=st["nlp%d" % h][:], in0=nbm[:, 2 * h:2 * h + 2, :],
-                                        in1=bank("lg%d" % h, [P, 2, A])[:], op=ALU.subtract)
-            return f
+        b3ps = psum.tile([P, 512], F32, name="b3ps", tag="bank")
+        nc.tensor.matmul(out=b3ps[:, 0:A], lhsT=ones[:], rhs=b3row[:], start=True, stop=True)
+        nc.vector.tensor_tensor(out=nbm[:], in0=nbm[:],
+                                in1=b3ps[:, 0:A].unsqueeze(1).to_broadcast([P, 8, A]), op=ALU.subtract)
 
-        def mk_mn(h):
-            def f():
-                st["nmx%d" % h] = sm.tile([P, 2], F32, name="nmx%d" % h, tag="nmx")
-                nc.vector.tensor_reduce(out=st["nmx%d" % h][:], in_=st["nlp%d" % h][:], axis=AX.X, op=ALU.min)
-            return f
-
-        def mk_ex(h):
-            def f():
-                st["e%d" % h] = sm.tile([P, 2, A], F32, name="e%d" % h, tag="e")
-                st["s%d" % h] = sm.tile([P, 2], F32, name="s%d" % h, tag="s")
-                for ii in range(2):
-                    nc.scalar.activation(out=st["e%d" % h][:, ii, :], in_=st["nlp%d" % h][:, ii, :], func=ACT.Exp,
-                                         bias=st["nmx%d" % h][:, ii:ii + 1], scale=-1.0,
-                                         accum_out=st["s%d" % h][:, ii:ii + 1])
-            return f
-
-        def mk_rc(h):
-            def f():
-                st["r%d" % h] = sm.tile([P, 2], F32, name="r%d" % h, tag="r")
-                nc.vector.reciprocal(out=st["r%d" % h][:], in_=st["s%d" % h][:])
-            return f
-
-        def mk_sc(h):
-            def f():
-                e = st["e%d" % h]
-                for ii in range(2):
-                    nc.scalar.activation(out=e[:, ii, :], in_=e[:, ii, :], func=ACT.Copy,
-                                         scale=st["r%d" % h][:, ii:ii + 1])
-                nc.sync.dma_start(out=out[256 * h:256 * h + 256, :].rearrange("(i p) a -> p i a", p=P), in_=e[:])
-            return f
-
-        for h in range(4):
-            deps = ["w3q"]
-            for u in range(len(UNITS)):
-                g, i0, nb = UNITS[u]
-                if i0 < 2 * h + 2 and 2 * h < i0 + nb:
-                    deps.append("qH%d" % u)
-            ops["m2.%d" % h] = (tuple(deps), mk_m2(h))
-            ops["nl%d" % h] = (("m2.%d" % h, "mask2"), mk_nl(h))
-            ops["mn%d" % h] = (("nl%d" % h,), mk_mn(h))
-            ops["ex%d" % h] = (("mn%d" % h,), mk_ex(h))
-            ops["rc%d" % h] = (("ex%d" % h,), mk_rc(h))
-            ops["sc%d" % h] = (("rc%d" % h,), mk_sc(h))
-
-        te = ["b2t"]
-        sc = []
-        ve = ["b2c", "b2o"] + ["gs%d" % i for i in range(8)] + ["mask2"]
-        for i in range(8):
-            for gp in range(2):
-                te.append("tr%d.%d" % (i, gp))
-                sc.append("ho%d.%d" % (i, gp))
-        ve += ["h1q%d.%d" % (bh, c) for bh in range(2) for c in range(4)]
-        te += ["p0.%d" % c for c in range(4)]
-        pieces = ["rS%d.%d" % (k, z) for k in range(16) for z in range(2)]
-        biases = ["bi%d.%d" % (u, t) for u in range(6) for t in range(4)]
-        sc += pieces[:AHEAD]
-        rest = pieces[AHEAD:]
-        for j in range(len(biases)):
-            sc.append(biases[j])
-            if j < len(rest):
-                sc.append(rest[j])
-        late = []
-        for u in range(6):
-            late += ["st%d" % u, "qH%d" % u]
-        for k in range(17):
-            if k < 16:
-                ve.append("rV%d" % k)
-            if k >= EFROM:
-                ve.append(late.pop(0))
-            if k == 13:
-                ve.append("w3r")
-            if k >= 1:
-                ve.append("qW%d" % (k - 1))
-            if k == 14:
-                ve.append("w3q")
-        ve += late
-        te += ["G%d.%d" % (u, t) for u in range(2, 9) for t in range(4)]
-        te += ["m2.0"] + ["G9.%d" % t for t in range(4)] + ["m2.1", "m2.2", "m2.3"]
-        sc += ["bi%d.%d" % (u, t) for u in range(6, 9) for t in range(4)]
-        sc += ["ex0"] + ["bi9.%d" % t for t in range(4)] + ["sc0", "ex1", "sc1", "ex2", "sc2", "ex3", "sc3"]
-        ve += ["st6", "qH6", "st7", "qH7", "nl0", "mn0", "st8", "qH8", "rc0", "nl1", "mn1",
-               "st9", "qH9", "rc1", "nl2", "mn2", "nl3", "mn3", "rc2", "rc3"]
-
-        queues = [te, sc, ve]
-        assert sum([len(q) for q in queues]) == len(ops)
-        pos = [0, 0, 0]
-        done = set()
-        moved = True
-        while moved:
-            moved = False
-            for qi in range(3):
-                while pos[qi] < len(queues[qi]) and all([d in done for d in ops[queues[qi][pos[qi]]][0]]):
-                    key = queues[qi][pos[qi]]
-                    ops[key][1]()
-                    done.add(key)
-                    pos[qi] += 1
-                    moved = True
-        assert len(done) == len(ops)
+        for k in range(4):
+            w2_chunk(k)
+        nxt = 4
+        waiting = []
+        heads = 0
+        covered = 0
+        for u in range(len(UNITS)):
+            waiting.append((u, mm1(u, u == 0)))
+            for z in range(2):
+                if nxt < 16:
+                    w2_chunk(nxt)
+                    nxt += 1
+            if len(waiting) > LAG:
+                (v, groups) = waiting.pop(0)
+                epilogue(v, groups)
+                if UNITS[v][0] == 3:
+                    covered += UNITS[v][2]
+            if u == 5:
+                w3g = const.tile([P, 4, A, 4], BF16, name="w3g", align_bytes=64)
+                nc.vector.tensor_copy(out=w3g[:], in_=w3raw[:].rearrange("p (g t) a -> p g a t", t=4))
+                nc.vector.quantize_mx(out=w3codes[:].bitcast(FP8X4), scales=w3sc[:],
+                                      in_=w3g[:].rearrange("p g a t -> p (g a t)"))
+            if True and covered >= HEAD * (heads + 2):
+                head(heads)
+                heads += 1
+        for (v, groups) in waiting:
+            epilogue(v, groups)
+        while heads * HEAD < 8:
+            head(heads)
+            heads += 1

@@ -18,7 +18,7 @@ SLOPE = 0.4
 BIG = 1.0e30
 FLOPS = 2 * B * H1 * H2 + 2 * B * H2 * A
 
-WVS = (320, 224, 224, 160)
+WVS = (288, 176, 176, 112)
 LAG = 1
 UNITS = [(0, 0, 4), (0, 4, 4), (1, 0, 4), (1, 4, 4), (2, 0, 4), (2, 4, 4), (3, 0, 2), (3, 2, 2), (3, 4, 2), (3, 6, 2)]
 HEAD = 2
@@ -251,7 +251,7 @@ def tile_dqn_pa_kernel(tc, x, h1, W2, b2, W3, b3, out):
                     covered += UNITS[v][2]
             if u == 5:
                 w3g = const.tile([P, 4, A, 4], BF16, name="w3g", align_bytes=64)
-                nc.vector.tensor_copy(out=w3g[:], in_=w3raw[:].rearrange("p (g t) a -> p g a t", t=4))
+                nc.scalar.copy(out=w3g[:], in_=w3raw[:].rearrange("p (g t) a -> p g a t", t=4))
                 nc.vector.quantize_mx(out=w3codes[:].bitcast(FP8X4), scales=w3sc[:],
                                       in_=w3g[:].rearrange("p g a t -> p (g a t)"))
             if True and covered >= HEAD * (heads + 2):

@@ -18,7 +18,7 @@ SLOPE = 0.4
 BIG = 1.0e30
 FLOPS = 2 * B * H1 * H2 + 2 * B * H2 * A
 
-WVS = (288, 176, 176, 112)
+WVS = (304, 192, 192, 128)
 LAG = 1
 UNITS = [(0, 0, 4), (0, 4, 4), (1, 0, 4), (1, 4, 4), (2, 0, 4), (2, 4, 4), (3, 0, 2), (3, 2, 2), (3, 4, 2), (3, 6, 2)]
 HEAD = 2
@@ -33,10 +33,21 @@ def tile_dqn_pa_kernel(tc, x, h1, W2, b2, W3, b3, out):
         w2gp = ctx.enter_context(tc.tile_pool(name="w2gp", bufs=4))
         h2gp = ctx.enter_context(tc.tile_pool(name="h2gp", bufs=2))
         sm = ctx.enter_context(tc.tile_pool(name="sm", bufs=2))
+        xtp = ctx.enter_context(tc.tile_pool(name="xtp", bufs=2))
         psum = ctx.enter_context(tc.psum_pool(name="psum", bufs=8))
 
         ident = const.tile([P, P], F32, name="ident")
         make_identity(nc, ident[:])
+        identb = const.tile([P, P], BF16, name="identb")
+        make_identity(nc, identb[:])
+        sel32 = const.tile([P, G, A], F32, name="sel32")
+        nc.gpsimd.memset(sel32[:], 1.0)
+        nc.gpsimd.affine_select(out=sel32[:], in_=sel32[:], pattern=[[P, G], [-G, A]], compare_op=ALU.is_ge,
+                                fill=0.0, base=0, channel_multiplier=1)
+        nc.gpsimd.affine_select(out=sel32[:], in_=sel32[:], pattern=[[-P, G], [G, A]], compare_op=ALU.is_ge,
+                                fill=0.0, base=G - 1, channel_multiplier=-1)
+        sel = const.tile([P, G, A], BF16, name="sel")
+        nc.vector.tensor_copy(out=sel[:], in_=sel32[:])
         warm = const.tile([P, 2], F32, name="warm")
         nc.vector.memset(warm[:], 0.0)
         nc.scalar.activation(out=warm[:, 1:2], in_=warm[:, 0:1], func=ACT.Exp)
@@ -209,13 +220,23 @@ def tile_dqn_pa_kernel(tc, x, h1, W2, b2, W3, b3, out):
             nc.sync.dma_start(out=out[rows * j:rows * (j + 1), :].rearrange("(i p) a -> p i a", p=P), in_=e[:])
 
         nbm = const.tile([P, 8, A], F32, name="nbm")
+        xrow = {}
         for (i0, n, t) in xparts:
             for i in range(n):
-                nc.vector.tensor_reduce(out=nbm[:, i0 + i, :],
-                                        in_=t[:, i, :].rearrange("p (a j) -> p a j", j=G),
-                                        axis=AX.X, op=ALU.add)
-        nc.vector.tensor_scalar(out=nbm[:], in0=nbm[:], scalar1=0.0, scalar2=BIG,
-                                op0=ALU.is_equal, op1=ALU.mult)
+                xrow[i0 + i] = t[:, i, :]
+        for j in range(2):
+            gs = psum.tile([P, 4, A], F32, name="gs%d" % j, tag="bank")
+            for ii in range(4):
+                xps = psum.tile([P, G, P], BF16, name="xps%d_%d" % (j, ii), tag="bank")
+                for f in range(G):
+                    nc.tensor.transpose(xps[:, f, :], xrow[4 * j + ii][:, f * P:(f + 1) * P], identb[:])
+                xT = xtp.tile([P, G, P], BF16, name="xT%d_%d" % (j, ii), tag="xT")
+                nc.scalar.copy(out=xT[:], in_=xps[:])
+                for f in range(G):
+                    nc.tensor.matmul(out=gs[:, ii, :], lhsT=xT[:, f, :], rhs=sel[:, f, :],
+                                     start=(f == 0), stop=(f == G - 1))
+            nc.vector.tensor_scalar(out=nbm[:, 4 * j:4 * j + 4, :], in0=gs[:], scalar1=0.0, scalar2=BIG,
+                                    op0=ALU.is_equal, op1=ALU.mult)
 
         h1_half(0)
         h1_half(1)

@@ -18,7 +18,7 @@ SLOPE = 0.4
 BIG = 1.0e30
 FLOPS = 2 * B * H1 * H2 + 2 * B * H2 * A
 
-WVS = (304, 192, 192, 128)
+WVS = (240, 128, 128, 64)
 LAG = 1
 UNITS = [(0, 0, 4), (0, 4, 4), (1, 0, 4), (1, 4, 4), (2, 0, 4), (2, 4, 4), (3, 0, 2), (3, 2, 2), (3, 4, 2), (3, 6, 2)]
 HEAD = 2
@@ -33,21 +33,10 @@ def tile_dqn_pa_kernel(tc, x, h1, W2, b2, W3, b3, out):
         w2gp = ctx.enter_context(tc.tile_pool(name="w2gp", bufs=4))
         h2gp = ctx.enter_context(tc.tile_pool(name="h2gp", bufs=2))
         sm = ctx.enter_context(tc.tile_pool(name="sm", bufs=2))
-        xtp = ctx.enter_context(tc.tile_pool(name="xtp", bufs=2))
         psum = ctx.enter_context(tc.psum_pool(name="psum", bufs=8))
 
         ident = const.tile([P, P], F32, name="ident")
         make_identity(nc, ident[:])
-        identb = const.tile([P, P], BF16, name="identb")
-        make_identity(nc, identb[:])
-        sel32 = const.tile([P, G, A], F32, name="sel32")
-        nc.gpsimd.memset(sel32[:], 1.0)
-        nc.gpsimd.affine_select(out=sel32[:], in_=sel32[:], pattern=[[P, G], [-G, A]], compare_op=ALU.is_ge,
-                                fill=0.0, base=0, channel_multiplier=1)
-        nc.gpsimd.affine_select(out=sel32[:], in_=sel32[:], pattern=[[-P, G], [G, A]], compare_op=ALU.is_ge,
-                                fill=0.0, base=G - 1, channel_multiplier=-1)
-        sel = const.tile([P, G, A], BF16, name="sel")
-        nc.vector.tensor_copy(out=sel[:], in_=sel32[:])
         warm = const.tile([P, 2], F32, name="warm")
         nc.vector.memset(warm[:], 0.0)
         nc.scalar.activation(out=warm[:, 1:2], in_=warm[:, 0:1], func=ACT.Exp)
@@ -220,23 +209,13 @@ def tile_dqn_pa_kernel(tc, x, h1, W2, b2, W3, b3, out):
             nc.sync.dma_start(out=out[rows * j:rows * (j + 1), :].rearrange("(i p) a -> p i a", p=P), in_=e[:])
 
         nbm = const.tile([P, 8, A], F32, name="nbm")
-        xrow = {}
         for (i0, n, t) in xparts:
             for i in range(n):
-                xrow[i0 + i] = t[:, i, :]
-        for j in range(2):
-            gs = psum.tile([P, 4, A], F32, name="gs%d" % j, tag="bank")
-            for ii in range(4):
-                xps = psum.tile([P, G, P], BF16, name="xps%d_%d" % (j, ii), tag="bank")
-                for f in range(G):
-                    nc.tensor.transpose(xps[:, f, :], xrow[4 * j + ii][:, f * P:(f + 1) * P], identb[:])
-                xT = xtp.tile([P, G, P], BF16, name="xT%d_%d" % (j, ii), tag="xT")
-                nc.scalar.copy(out=xT[:], in_=xps[:])
-                for f in range(G):
-                    nc.tensor.matmul(out=gs[:, ii, :], lhsT=xT[:, f, :], rhs=sel[:, f, :],
-                                     start=(f == 0), stop=(f == G - 1))
-            nc.vector.tensor_scalar(out=nbm[:, 4 * j:4 * j + 4, :], in0=gs[:], scalar1=0.0, scalar2=BIG,
-                                    op0=ALU.is_equal, op1=ALU.mult)
+                nc.vector.tensor_reduce(out=nbm[:, i0 + i, :],
+                                        in_=t[:, i, :].rearrange("p (a j) -> p a j", j=G),
+                                        axis=AX.X, op=ALU.add)
+        nc.vector.tensor_scalar(out=nbm[:], in0=nbm[:], scalar1=0.0, scalar2=BIG,
+                                op0=ALU.is_equal, op1=ALU.mult)
 
         h1_half(0)
         h1_half(1)

from contextlib import ExitStack

import concourse.mybir as mybir
from concourse.masks import make_identity

F32 = mybir.dt.float32
BF16 = mybir.dt.bfloat16
U32 = mybir.dt.uint32
U8 = mybir.dt.uint8
FP8X4 = mybir.dt.float8_e4m3fn_x4
ALU = mybir.AluOpType
ACT = mybir.ActivationFunctionType
AX = mybir.AxisListType

P = 128
B, A, G, H1, H2 = 1024, 128, 5, 2048, 2048
SLOPE = 0.4
BIG = 1.0e30
FLOPS = 2 * B * H1 * H2 + 2 * B * H2 * A

WVS = (240, 128, 128, 64)
LAG = 1
UNITS = [(0, 0, 4), (0, 4, 4), (1, 0, 4), (1, 4, 4), (2, 0, 4), (2, 4, 4), (3, 0, 2), (3, 2, 2), (3, 4, 2), (3, 6, 2)]
HEAD = 2


def tile_dqn_pa_kernel(tc, x, h1, W2, b2, W3, b3, out):
    nc = tc.nc
    with ExitStack() as ctx:
        const = ctx.enter_context(tc.tile_pool(name="const", bufs=1))
        raw = ctx.enter_context(tc.tile_pool(name="raw", bufs=12))
        big = ctx.enter_context(tc.tile_pool(name="big", bufs=5))
        w2gp = ctx.enter_context(tc.tile_pool(name="w2gp", bufs=4))
        h2gp = ctx.enter_context(tc.tile_pool(name="h2gp", bufs=2))
        sm = ctx.enter_context(tc.tile_pool(name="sm", bufs=2))
        psum = ctx.enter_context(tc.psum_pool(name="psum", bufs=8))

        ident = const.tile([P, P], F32, name="ident")
        make_identity(nc, ident[:])
        warm = const.tile([P, 2], F32, name="warm")
        nc.vector.memset(warm[:], 0.0)
        nc.scalar.activation(out=warm[:, 1:2], in_=warm[:, 0:1], func=ACT.Exp)
        b2rows = const.tile([P, P], BF16, name="b2rows")
        nc.vector.memset(b2rows[:], 0.0)
        nc.scalar.dma_start(out=b2rows[0:16, :], in_=b2.rearrange("(m p) -> m p", p=P))
        b3row = const.tile([P, A], BF16, name="b3row")
        nc.vector.memset(b3row[:], 0.0)
        ones = const.tile([P, P], BF16, name="ones")
        nc.vector.memset(ones[:], 1.0)

        h1codes = const.tile([P, 4, B], U32, name="h1codes", align_bytes=64)
        h1sc = const.tile([P, 4, B], U8, name="h1sc", align_bytes=64)
        w2codes = const.tile([P, 4, H2], U32, name="w2codes", align_bytes=64)
        w2sc = const.tile([P, 4, H2], U8, name="w2sc", align_bytes=64)
        h2codes = const.tile([P, 4, B], U32, name="h2codes", align_bytes=64)
        h2sc = const.tile([P, 4, B], U8, name="h2sc", align_bytes=64)
        w3codes = const.tile([P, 4 * A], U32, name="w3codes", align_bytes=64)
        w3sc = const.tile([P, 4 * A], U8, name="w3sc", align_bytes=64)

        xparts = []
        h1raw = []

        def load_x(i0, n):
            t = raw.tile([P, n, A * G], BF16, name="xraw%d" % i0, tag="raw")
            nc.sync.dma_start(out=t[:], in_=x[i0 * P:(i0 + n) * P, :].rearrange("(i p) c -> p i c", p=P))
            xparts.append((i0, n, t))

        def load_h1(i):
            t = raw.tile([P, H1], BF16, name="h1raw%d" % i, tag="raw")
            nc.sync.dma_start(out=t[:], in_=h1[i * P:(i + 1) * P, :])
            h1raw.append(t)

        load_h1(0)
        load_x(0, 3)
        load_h1(1)
        load_h1(2)
        load_x(3, 3)
        load_h1(3)
        load_h1(4)
        load_x(6, 2)
        for i in range(5, 8):
            load_h1(i)
        nc.sync.dma_start(out=b3row[0:1, :], in_=b3.rearrange("(o a) -> o a", o=1))
        w2raw = []
        for k in range(16):
            g, c = k // 4, k % 4
            t = raw.tile([P, 4, 512], BF16, name="w2raw%d" % k, tag="raw")
            for u in range(2):
                r0 = 512 * c + 256 * u
                nc.sync.dma_start(
                    out=t[:, 2 * u:2 * u + 2, :],
                    in_=W2[r0:r0 + 256, 512 * g:512 * g + 512].rearrange("(q e) w -> q e w", e=2),
                )
            w2raw.append(t)
        w3raw = raw.tile([P, 16, A], BF16, name="w3raw", tag="raw")
        nc.sync.dma_start(out=w3raw[:], in_=W3.rearrange("(m p) a -> p m a", p=P))

        def h1_half(bh):
            units = [
                big.tile([P, 2 * 512 * 4], BF16, name="h1g%d_%d" % (bh, gp), tag="big", align_bytes=64)
                for gp in range(2)
            ]
            for ii in range(4):
                words = h1raw[4 * bh + ii][:].bitcast(F32)
                for gp in range(2):
                    bank = psum.tile([P, 2, 2, P], F32, name="trb%d_%d_%d" % (bh, ii, gp), tag="bank")
                    for gg in range(2):
                        for u in range(2):
                            w0 = 256 * (2 * gp + gg) + 128 * u
                            nc.tensor.transpose(bank[:, gg, u, :], words[:, w0:w0 + P], ident[:])
                    dst = units[gp][:].bitcast(F32).rearrange("p (g b u) -> p g b u", g=2, u=2)
                    dst = dst[:, :, ii * P:(ii + 1) * P, :]
                    nc.scalar.copy(out=dst, in_=bank[:].rearrange("p g u b -> p g b u"))
            for c in range(4):
                nc.vector.quantize_mx(
                    out=h1codes[:, c, 512 * bh:512 * bh + 512].bitcast(FP8X4),
                    scales=h1sc[:, c, 512 * bh:512 * bh + 512],
                    in_=units[c // 2][:, 2048 * (c % 2):2048 * (c % 2) + 2048],
                )

        def w2_chunk(k):
            g, c = k // 4, k % 4
            wv = WVS[g]
            src = w2raw[k]
            grp = w2gp.tile([P, 512, 4], BF16, name="w2g%d" % k, tag="w2g", align_bytes=64)
            nc.vector.tensor_copy(
                out=grp[:, 0:wv, :].rearrange("p (c i) t -> p c t i", i=4),
                in_=src[:, :, 0:wv].rearrange("p t (c i) -> p c t i", i=4),
            )
            nc.scalar.copy(
                out=grp[:, wv:512, :].rearrange("p (c i) t -> p c t i", i=4),
                in_=src[:, :, wv:512].rearrange("p t (c i) -> p c t i", i=4),
            )
            nc.vector.quantize_mx(
                out=w2codes[:, c, 512 * g:512 * g + 512].bitcast(FP8X4),
                scales=w2sc[:, c, 512 * g:512 * g + 512],
                in_=grp[:].rearrange("p w t -> p (w t)"),
            )

        def mm1(u, c_outer):
            g, i0, nb = UNITS[u]
            n = P * nb
            per = 512 // n
            banks = [psum.tile([P, per, n], F32, name="mm%d_%d" % (u, j), tag="bank") for j in range(4 // per)]
            groups = [banks[t // per][:, t % per, :] for t in range(4)]
            if c_outer:
                order = [(c, t) for c in range(4) for t in range(4)]
            else:
                order = [(c, t) for t in range(4) for c in range(4)]
            for (c, t) in order:
                m = 4 * g + t
                nc.tensor.matmul_mx(
                    out=groups[t],
                    lhsT=w2codes[:, c, m * P:(m + 1) * P].bitcast(FP8X4),
                    lhsT_scale=w2sc[:, c, m * P:(m + 1) * P],
                    rhs=h1codes[:, c, P * i0:P * i0 + n].bitcast(FP8X4),
                    rhs_scale=h1sc[:, c, P * i0:P * i0 + n],
                    start=(c == 0),
                    stop=(c == 3),
                )
            return groups

        def epilogue(u, groups):
            g, i0, nb = UNITS[u]
            n = P * nb
            a = big.tile([P, 4, n], F32, name="a%d" % u, tag="big", align_bytes=64)
            for t in range(4):
                m = 4 * g + t
                nc.scalar.activation(out=a[:, t, :], in_=groups[t], func=ACT.Identity,
                                     bias=b2T[:, m:m + 1], scale=1.0)
            h2g = h2gp.tile([P, n, 4], BF16, name="h2g%d" % u, tag="h2g", align_bytes=64)
            av = a[:].rearrange("p t b -> p b t")
            nc.vector.scalar_tensor_tensor(out=h2g[:], in0=av, scalar=SLOPE, in1=av,
                                           op0=ALU.mult, op1=ALU.max)
            nc.vector.quantize_mx(
                out=h2codes[:, g, P * i0:P * i0 + n].bitcast(FP8X4),
                scales=h2sc[:, g, P * i0:P * i0 + n],
                in_=h2g[:].rearrange("p b t -> p (b t)"),
            )

        def head(j):
            lg = psum.tile([P, HEAD, A], F32, name="lg%d" % j, tag="bank")
            for ii in range(HEAD):
                i = HEAD * j + ii
                for g in range(4):
                    nc.tensor.matmul_mx(
                        out=lg[:, ii, :],
                        lhsT=h2codes[:, g, i * P:(i + 1) * P].bitcast(FP8X4),
                        lhsT_scale=h2sc[:, g, i * P:(i + 1) * P],
                        rhs=w3codes[:, g * A:(g + 1) * A].bitcast(FP8X4),
                        rhs_scale=w3sc[:, g * A:(g + 1) * A],
                        start=(g == 0),
                        stop=(g == 3),
                    )
            nlp = sm.tile([P, HEAD, A], F32, name="nlp%d" % j, tag="nlp")
            nc.vector.tensor_tensor(out=nlp[:], in0=nbm[:, HEAD * j:HEAD * (j + 1), :], in1=lg[:], op=ALU.subtract)
            nmx = sm.tile([P, HEAD], F32, name="nmx%d" % j, tag="nmx")
            nc.vector.tensor_reduce(out=nmx[:], in_=nlp[:], axis=AX.X, op=ALU.min)
            e = sm.tile([P, HEAD, A], F32, name="e%d" % j, tag="e")
            s = sm.tile([P, HEAD], F32, name="s%d" % j, tag="s")
            for ii in range(HEAD):
                nc.scalar.activation(out=e[:, ii, :], in_=nlp[:, ii, :], func=ACT.Exp,
                                     bias=nmx[:, ii:ii + 1], scale=-1.0, accum_out=s[:, ii:ii + 1])
            r = sm.tile([P, HEAD], F32, name="r%d" % j, tag="r")
            nc.vector.reciprocal(out=r[:], in_=s[:])
            for ii in range(HEAD):
                nc.scalar.activation(out=e[:, ii, :], in_=e[:, ii, :], func=ACT.Copy, scale=r[:, ii:ii + 1])
            rows = P * HEAD
            nc.sync.dma_start(out=out[rows * j:rows * (j + 1), :].rearrange("(i p) a -> p i a", p=P), in_=e[:])

        nbm = const.tile([P, 8, A], F32, name="nbm")
        for (i0, n, t) in xparts:
            for i in range(n):
                nc.vector.tensor_reduce(out=nbm[:, i0 + i, :],
                                        in_=t[:, i, :].rearrange("p (a j) -> p a j", j=G),
                                        axis=AX.X, op=ALU.add)
        nc.vector.tensor_scalar(out=nbm[:], in0=nbm[:], scalar1=0.0, scalar2=BIG,
                                op0=ALU.is_equal, op1=ALU.mult)

        h1_half(0)
        h1_half(1)

        b2rows32 = const.tile([P, P], F32, name="b2rows32")
        nc.vector.tensor_copy(out=b2rows32[:], in_=b2rows[:])
        b2ps = psum.tile([P, 512], F32, name="b2ps", tag="bank")
        nc.tensor.transpose(b2ps[:, 0:P], b2rows32[:], ident[:])
        b2T = const.tile([P, 16], F32, name="b2T")
        nc.vector.tensor_copy(out=b2T[:], in_=b2ps[:, 0:16])

        b3ps = psum.tile([P, 512], F32, name="b3ps", tag="bank")
        nc.tensor.matmul(out=b3ps[:, 0:A], lhsT=ones[:], rhs=b3row[:], start=True, stop=True)
        nc.vector.tensor_tensor(out=nbm[:], in0=nbm[:],
                                in1=b3ps[:, 0:A].unsqueeze(1).to_broadcast([P, 8, A]), op=ALU.subtract)

        for k in range(4):
            w2_chunk(k)
        nxt = 4
        waiting = []
        heads = 0
        covered = 0
        for u in range(len(UNITS)):
            waiting.append((u, mm1(u, u == 0)))
            for z in range(2):
                if nxt < 16:
                    w2_chunk(nxt)
                    nxt += 1
            if len(waiting) > LAG:
                (v, groups) = waiting.pop(0)
                epilogue(v, groups)
                if UNITS[v][0] == 3:
                    covered += UNITS[v][2]
            if u == 5:
                w3g = const.tile([P, 4, A, 4], BF16, name="w3g", align_bytes=64)
                nc.scalar.copy(out=w3g[:], in_=w3raw[:].rearrange("p (g t) a -> p g a t", t=4))
                nc.vector.quantize_mx(out=w3codes[:].bitcast(FP8X4), scales=w3sc[:],
                                      in_=w3g[:].rearrange("p g a t -> p (g a t)"))
            if True and covered >= HEAD * (heads + 2):
                head(heads)
                heads += 1
        for (v, groups) in waiting:
            epilogue(v, groups)
        while heads * HEAD < 8:
            head(heads)
            heads += 1
